import numpy as np
import ml_dtypes


BF16 = ml_dtypes.bfloat16


def bf(x):
    return np.asarray(x, np.float32).astype(BF16)


def f64(x):
    return np.asarray(x).astype(np.float64)


E2M1 = np.array([0.0, 0.5, 1.0, 1.5, 2.0, 3.0, 4.0, 6.0, -0.0, -0.5, -1.0, -1.5, -2.0, -3.0, -4.0, -6.0])


def pack_weight(w, fmt):
    k, n = w.shape
    w = f64(bf(w)).reshape(k // 32, 32, n)
    amax = np.abs(w).max(1)
    if fmt == "e4m3":
        byte = np.frexp(amax)[1] - 1 + 127 - 7
    else:
        mant, ex = np.frexp(amax / 6.0)
        byte = np.where(mant > 0.5, ex, ex - 1) + 127
    byte = np.clip(np.where(amax > 0, byte, 1), 1, 254)
    scaled = (w * np.exp2(127.0 - byte)[:, None, :]).reshape(k, n).astype(np.float32)
    by_word = np.ascontiguousarray(scaled.reshape(k // 512, 128, 4, n).transpose(0, 1, 3, 2))
    if fmt == "e4m3":
        words = by_word.astype(ml_dtypes.float8_e4m3fn).view(np.uint8)
    else:
        c = by_word.astype(ml_dtypes.float4_e2m1fn).view(np.uint8) & 0xF
        words = c[..., 0::2] | (c[..., 1::2] << 4)
    return np.ascontiguousarray(words), np.ascontiguousarray(byte.astype(np.uint8).reshape(k // 512, 16, n))


def unpack_weight(words, scales, fmt):
    g, p, n, _ = words.shape
    if fmt == "e4m3":
        vals = np.ascontiguousarray(words).view(ml_dtypes.float8_e4m3fn).astype(np.float64)
    else:
        nib = np.empty((g, p, n, 4), np.uint8)
        nib[..., 0::2] = words & 0xF
        nib[..., 1::2] = words >> 4
        vals = E2M1[nib]
    vals = vals * np.repeat(np.exp2(scales.astype(np.float64) - 127.0), 8, axis=1)[..., None]
    return vals.transpose(0, 1, 3, 2).reshape(g * 512, n)

def pack4(w):
    words, scales = pack_weight(w, "e2m1")
    return words.reshape(words.shape[0], 128, -1), scales


def unpack4(words, scales):
    return unpack_weight(words.reshape(words.shape[0], 128, -1, 2), scales, "e2m1")


def kspread(k):
    return np.exp2(np.repeat(np.random.randint(-6, 7, k // 32), 32).astype(np.float64))


B, S, E, H, D = 4, 512, 4096, 8, 64
NH = 2 * H
P = NH * D
BASE = 10000.0


def rotary(t):
    inv_freq = 1.0 / BASE ** (np.arange(0, D, 2) / D)
    freqs = np.repeat(np.arange(S)[:, None] * inv_freq[None, :], 2, axis=-1)
    cos = np.cos(freqs)[None, :, None, :]
    sin = np.sin(freqs)[None, :, None, :]
    x = t.reshape(t.shape[:-1] + (D // 2, 2))
    x1, x2 = x[..., 0], x[..., 1]
    rot = np.stack([-x2, x1], axis=-1).reshape(t.shape)
    return t * cos + rot * sin


def setup_inputs():
    s = kspread(E)
    x = np.random.standard_normal((B, S, E)) * s
    x_words, x_scales = pack4(x.reshape(B * S, E).T)
    Wq_words, Wq_scales = pack4(np.random.standard_normal((E, P)) / np.sqrt(E) / s[:, None])
    Wk_words, Wk_scales = pack4(np.random.standard_normal((E, P)) / np.sqrt(E) / s[:, None])
    return {'x_words': x_words, 'x_scales': x_scales,
            'Wq_words': Wq_words, 'Wq_scales': Wq_scales,
            'Wk_words': Wk_words, 'Wk_scales': Wk_scales}


def reference(x_words, x_scales, Wq_words, Wq_scales, Wk_words, Wk_scales):
    xq = unpack4(x_words, x_scales).T.reshape(B, S, E)
    q = (xq @ unpack4(Wq_words, Wq_scales)).reshape(B, S, NH, D)
    k = (xq @ unpack4(Wk_words, Wk_scales)).reshape(B, S, NH, D)
    return rotary(q), rotary(k)

@@ -1,0 +1,184 @@
+import math
+from contextlib import ExitStack
+
+import concourse.mybir as mybir
+
+F32 = mybir.dt.float32
+I32 = mybir.dt.int32
+U8 = mybir.dt.uint8
+FP4X4 = mybir.dt.float4_e2m1fn_x4
+ALU = mybir.AluOpType
+SIN = mybir.ActivationFunctionType.Sin
+
+B, S, E, NH, D = 4, 512, 4096, 16, 64
+TOKENS = B * S
+C = NH * D
+BASE = 10000.0
+FLOPS = 2 * TOKENS * E * 2 * C
+
+P = 128
+G = E // 512
+N = 512
+HALF = D // 2
+POS_TILES = S // P
+
+
+def load_codes(nc, dst, words, g0, g1, c0, c1):
+    src = words[g0:g1, :, 2 * c0 : 2 * c1].rearrange("g p c -> p g c")
+    nc.sync.dma_start(out=dst[:].bitcast(I32), in_=src.bitcast(I32))
+
+
+def load_scales(nc, dst, scales, g0, g1, c0, c1):
+    for q in range(4):
+        src = scales[g0:g1, 4 * q : 4 * q + 4, c0:c1].rearrange("g r n -> r g n")
+        nc.sync.dma_start(out=dst[32 * q : 32 * q + 4, :, :].bitcast(I32), in_=src.bitcast(I32))
+
+
+def tile_multiheadflashdiff_pa_kernel(tc, x_words, x_scales, wq_words, wq_scales, wk_words, wk_scales, out_q, out_k):
+    nc = tc.nc
+    outs = [out_q.rearrange("b s h d -> (b s) (h d)"), out_k.rearrange("b s h d -> (b s) (h d)")]
+
+    with ExitStack() as ctx:
+        keep = ctx.enter_context(tc.tile_pool(name="keep", bufs=1))
+        work = ctx.enter_context(tc.tile_pool(name="work", bufs=4))
+        psum = ctx.enter_context(tc.psum_pool(name="psum", bufs=8))
+        ctx.enter_context(tc.manual_schedule())
+
+        def keep_tile(shape, dtype, name):
+            return keep.tile(shape, dtype, name=name, align_bytes=256)
+
+        codes = {}
+        planes = {}
+
+        def make_codes(op, words, g0, g1, c0, c1):
+            t = keep_tile([P, g1 - g0, 2 * (c1 - c0)], U8, "codes_%s_%d_%d" % (op, g0, c0))
+            load_codes(nc, t, words, g0, g1, c0, c1)
+            for g in range(g0, g1):
+                codes[op, g] = (t, g - g0)
+
+        def make_planes(op, g0, g1, c0, c1, engine):
+            t = keep_tile([P, g1 - g0, c1 - c0], U8, "planes_%s_%d_%d" % (op, g0, c0))
+            engine.memset(t[:].bitcast(I32), 0)
+            for g in range(g0, g1):
+                planes[op, g] = (t, g - g0)
+            return t
+
+        pos = keep_tile([P, POS_TILES, 1], F32, "pos")
+        nc.gpsimd.iota(pos[:], [[P, POS_TILES], [1, 1]], base=0, channel_multiplier=1, allow_small_or_imprecise_dtypes=True)
+        xp0 = make_planes("x0", 0, 2, 0, S, nc.vector)
+        qp0 = make_planes("q", 0, 2, 0, C, nc.vector)
+        xp1 = make_planes("x0", 2, G, 0, S, nc.vector)
+        qp1 = make_planes("q", 2, G, 0, C, nc.gpsimd)
+        kp = make_planes("k", 0, G, 0, C, nc.gpsimd)
+        rp = make_planes("x1", 0, G, S, TOKENS, nc.gpsimd)
+
+        make_codes("x0", x_words, 0, 1, 0, S)
+        make_codes("q", wq_words, 0, 1, 0, C)
+        load_scales(nc, xp0, x_scales, 0, 2, 0, S)
+        load_scales(nc, qp0, wq_scales, 0, 2, 0, C)
+        make_codes("x0", x_words, 1, 2, 0, S)
+        make_codes("q", wq_words, 1, 2, 0, C)
+        make_codes("x0", x_words, 2, 4, 0, S)
+        make_codes("q", wq_words, 2, 4, 0, C)
+        load_scales(nc, xp1, x_scales, 2, G, 0, S)
+        load_scales(nc, qp1, wq_scales, 2, G, 0, C)
+        make_codes("x0", x_words, 4, G, 0, S)
+        make_codes("q", wq_words, 4, 6, 0, C)
+        make_codes("q", wq_words, 6, G, 0, C)
+        load_scales(nc, kp, wk_scales, 0, G, 0, C)
+        for g in range(0, G, 2):
+            make_codes("k", wk_words, g, g + 2, 0, C)
+        load_scales(nc, rp, x_scales, 0, G, S, TOKENS)
+        for g in range(0, G, 2):
+            make_codes("x1", x_words, g, g + 2, S, TOKENS)
+
+        turns = keep_tile([P, 2, POS_TILES, HALF], F32, "turns")
+        whole = keep_tile([P, 2, POS_TILES, HALF], I32, "whole")
+        frac = keep_tile([P, 2, POS_TILES, HALF], F32, "frac")
+        cos_t = keep_tile([P, POS_TILES, HALF, 2], F32, "cos_t")
+        sin_t = keep_tile([P, POS_TILES, HALF, 2], F32, "sin_t")
+        nc.vector.tensor_scalar(out=turns[:, 0, :, 0:1], in0=pos[:], scalar1=1.0 / (2.0 * math.pi), scalar2=None, op0=ALU.mult)
+        w = 1
+        while w < HALF:
+            nc.vector.tensor_scalar(out=turns[:, 0, :, w : 2 * w], in0=turns[:, 0, :, 0:w], scalar1=BASE ** (-w / HALF), scalar2=None, op0=ALU.mult)
+            w = 2 * w
+        nc.vector.tensor_scalar(out=turns[:, 1, :, :], in0=turns[:, 0, :, :], scalar1=0.25, scalar2=None, op0=ALU.add)
+        nc.vector.tensor_copy(out=whole[:], in_=turns[:])
+        nc.vector.tensor_tensor(out=frac[:], in0=turns[:], in1=whole[:], op=ALU.subtract)
+        two_pi = 2.0 * math.pi
+        for t in range(2):
+            nc.scalar.activation(out=cos_t[:, :, :, t], in_=frac[:, 1, :, :], func=SIN, scale=two_pi)
+            nc.scalar.activation(out=sin_t[:, :, :, t], in_=frac[:, 0, :, :], func=SIN, scale=(two_pi if t == 1 else -two_pi))
+
+        def matmul(acc, tt, cb, c0, width, g):
+            xop, col = ("x0", tt) if tt < POS_TILES else ("x1", tt - POS_TILES)
+            wop, n0 = ("q" if cb < 2 else "k"), (cb % 2) * N + c0
+            xc, xi = codes[xop, g]
+            xs, xsi = planes[xop, g]
+            wc, wi = codes[wop, g]
+            ws, wsi = planes[wop, g]
+            nc.tensor.matmul_mx(
+                out=acc[:, 0:width],
+                lhsT=xc[:, xi, 2 * P * col : 2 * P * (col + 1)].bitcast(FP4X4),
+                lhsT_scale=xs[:, xsi, P * col : P * (col + 1)],
+                rhs=wc[:, wi, 2 * n0 : 2 * (n0 + width)].bitcast(FP4X4),
+                rhs_scale=ws[:, wsi, n0 : n0 + width],
+                start=(g == 0),
+                stop=(g == G - 1),
+            )
+
+        pending = []
+
+        def finish(engine):
+            a, b, tt, cb, c0, width = pending.pop(0)
+            o = work.tile([P, N], F32, name="o")
+            engine.tensor_tensor(out=o[:, 0:width], in0=a[:, 0:width], in1=b[:, 0:width], op=ALU.add)
+            n0 = (cb % 2) * N + c0
+            nc.sync.dma_start(out=outs[cb // 2][P * tt : P * (tt + 1), n0 : n0 + width], in_=o[:, 0:width])
+
+        def rotate(acc, tt, cb, c0, width):
+            heads = width // D
+            m = tt % POS_TILES
+            cosb = cos_t[:, m, :, :].rearrange("p j t -> p (j t)").unsqueeze(1).to_broadcast([P, heads, D])
+            sinb = sin_t[:, m, :, :].unsqueeze(1).to_broadcast([P, heads, HALF, 2])
+            a = work.tile([P, N], F32, name="a")
+            b = work.tile([P, N], F32, name="b")
+            nc.vector.tensor_tensor(
+                out=a[:, 0:width].rearrange("p (h d) -> p h d", d=D),
+                in0=acc[:, 0:width].rearrange("p (h d) -> p h d", d=D), in1=cosb, op=ALU.mult)
+            nc.vector.tensor_tensor(
+                out=b[:, 0:width].rearrange("p (h j t) -> p h j t", t=2, j=HALF),
+                in0=acc[:, 0:width].rearrange("p (h j t) -> p h j t", t=2, j=HALF)[:, :, :, ::-1], in1=sinb, op=ALU.mult)
+            pending.append((a, b, tt, cb, c0, width))
+
+        def new_acc():
+            return psum.tile([P, N], F32, name="acc")
+
+        first = [(tt, cb) for tt in range(POS_TILES) for cb in range(2)]
+        accs = [new_acc() for pair in first]
+        for g in range(G):
+            for acc, (tt, cb) in zip(accs, first):
+                matmul(acc, tt, cb, 0, N, g)
+        for acc, (tt, cb) in zip(accs, first):
+            rotate(acc, tt, cb, 0, N)
+            if len(pending) > 1:
+                finish(nc.vector)
+
+        rest = [(tt, cb) for tt in range(POS_TILES) for cb in range(2, 4)]
+        rest += [(tt, cb) for tt in range(POS_TILES, TOKENS // P) for cb in range(4)]
+        widths = {rest[-2]: [256, 256], rest[-1]: [256, 128, 128]}
+        for i, (tt, cb) in enumerate(rest):
+            c0 = 0
+            for width in widths.get((tt, cb), [N]):
+                acc = new_acc()
+                for g in range(G):
+                    matmul(acc, tt, cb, c0, width, g)
+                rotate(acc, tt, cb, c0, width)
+                c0 += width
+                tail = i >= len(rest) - 3
+                if tail:
+                    while len(pending) > 1:
+                        finish(nc.vector)
+                    finish(nc.vector if (i == len(rest) - 1 and c0 == N) else nc.gpsimd)
+                elif len(pending) > 1:
+                    finish(nc.vector)

@@ -6,6 +6,7 @@ import concourse.mybir as mybir
 F32 = mybir.dt.float32
 I32 = mybir.dt.int32
 U8 = mybir.dt.uint8
+BF16 = mybir.dt.bfloat16
 FP4X4 = mybir.dt.float4_e2m1fn_x4
 ALU = mybir.AluOpType
 SIN = mybir.ActivationFunctionType.Sin
@@ -40,7 +41,9 @@ def tile_multiheadflashdiff_pa_kernel(tc, x_words, x_scales, wq_words, wq_scales
 
     with ExitStack() as ctx:
         keep = ctx.enter_context(tc.tile_pool(name="keep", bufs=1))
-        work = ctx.enter_context(tc.tile_pool(name="work", bufs=4))
+        work = ctx.enter_context(tc.tile_pool(name="work", bufs=3))
+        store = ctx.enter_context(tc.tile_pool(name="store", bufs=5))
+        stage = ctx.enter_context(tc.tile_pool(name="stage", bufs=6))
         psum = ctx.enter_context(tc.psum_pool(name="psum", bufs=8))
         ctx.enter_context(tc.manual_schedule())
 
@@ -54,43 +57,41 @@ def tile_multiheadflashdiff_pa_kernel(tc, x_words, x_scales, wq_words, wq_scales
             t = keep_tile([P, g1 - g0, 2 * (c1 - c0)], U8, "codes_%s_%d_%d" % (op, g0, c0))
             load_codes(nc, t, words, g0, g1, c0, c1)
             for g in range(g0, g1):
-                codes[op, g] = (t, g - g0)
+                for c in range(c0, c1, N):
+                    codes[op, g, c // N] = (t, g - g0, c0)
 
-        def make_planes(op, g0, g1, c0, c1, engine):
+        def make_planes(op, g0, g1, c0, c1):
             t = keep_tile([P, g1 - g0, c1 - c0], U8, "planes_%s_%d_%d" % (op, g0, c0))
-            engine.memset(t[:].bitcast(I32), 0)
+            nc.vector.memset(t[:].bitcast(I32), 0)
             for g in range(g0, g1):
                 planes[op, g] = (t, g - g0)
             return t
 
         pos = keep_tile([P, POS_TILES, 1], F32, "pos")
         nc.gpsimd.iota(pos[:], [[P, POS_TILES], [1, 1]], base=0, channel_multiplier=1, allow_small_or_imprecise_dtypes=True)
-        xp0 = make_planes("x0", 0, 2, 0, S, nc.vector)
-        qp0 = make_planes("q", 0, 2, 0, C, nc.vector)
-        xp1 = make_planes("x0", 2, G, 0, S, nc.vector)
-        qp1 = make_planes("q", 2, G, 0, C, nc.gpsimd)
-        kp = make_planes("k", 0, G, 0, C, nc.gpsimd)
-        rp = make_planes("x1", 0, G, S, TOKENS, nc.gpsimd)
+        xp0 = make_planes("x0", 0, 4, 0, S)
+        dummy = keep_tile([P, N], BF16, "dummy")
+        nc.vector.memset(dummy[:].bitcast(I32), 0)
+        qp0 = make_planes("q", 0, 2, 0, C)
+        qp1 = make_planes("q", 2, 4, 0, C)
+        xp1 = make_planes("x0", 4, G, 0, S)
+        qp2 = make_planes("q", 4, G, 0, C)
 
         make_codes("x0", x_words, 0, 1, 0, S)
-        make_codes("q", wq_words, 0, 1, 0, C)
-        load_scales(nc, xp0, x_scales, 0, 2, 0, S)
+        make_codes("q", wq_words, 0, 1, 0, N)
+        load_scales(nc, xp0, x_scales, 0, 4, 0, S)
         load_scales(nc, qp0, wq_scales, 0, 2, 0, C)
+        make_codes("q", wq_words, 0, 1, N, C)
         make_codes("x0", x_words, 1, 2, 0, S)
         make_codes("q", wq_words, 1, 2, 0, C)
         make_codes("x0", x_words, 2, 4, 0, S)
         make_codes("q", wq_words, 2, 4, 0, C)
-        load_scales(nc, xp1, x_scales, 2, G, 0, S)
-        load_scales(nc, qp1, wq_scales, 2, G, 0, C)
+        load_scales(nc, qp1, wq_scales, 2, 4, 0, C)
         make_codes("x0", x_words, 4, G, 0, S)
         make_codes("q", wq_words, 4, 6, 0, C)
+        load_scales(nc, xp1, x_scales, 4, G, 0, S)
+        load_scales(nc, qp2, wq_scales, 4, G, 0, C)
         make_codes("q", wq_words, 6, G, 0, C)
-        load_scales(nc, kp, wk_scales, 0, G, 0, C)
-        for g in range(0, G, 2):
-            make_codes("k", wk_words, g, g + 2, 0, C)
-        load_scales(nc, rp, x_scales, 0, G, S, TOKENS)
-        for g in range(0, G, 2):
-            make_codes("x1", x_words, g, g + 2, S, TOKENS)
 
         turns = keep_tile([P, 2, POS_TILES, HALF], F32, "turns")
         whole = keep_tile([P, 2, POS_TILES, HALF], I32, "whole")
@@ -110,75 +111,99 @@ def tile_multiheadflashdiff_pa_kernel(tc, x_words, x_scales, wq_words, wq_scales
             nc.scalar.activation(out=cos_t[:, :, :, t], in_=frac[:, 1, :, :], func=SIN, scale=two_pi)
             nc.scalar.activation(out=sin_t[:, :, :, t], in_=frac[:, 0, :, :], func=SIN, scale=(two_pi if t == 1 else -two_pi))
 
+        kp = make_planes("k", 0, G, 0, C)
+        load_scales(nc, kp, wk_scales, 0, G, 0, C)
+        for g in range(0, G, 2):
+            make_codes("k", wk_words, g, g + 2, 0, C)
+        rp = make_planes("x1", 0, G, S, TOKENS)
+        load_scales(nc, rp, x_scales, 0, G, S, TOKENS)
+        for g in range(0, G, 2):
+            make_codes("x1", x_words, g, g + 2, S, TOKENS)
+
         def matmul(acc, tt, cb, c0, width, g):
             xop, col = ("x0", tt) if tt < POS_TILES else ("x1", tt - POS_TILES)
             wop, n0 = ("q" if cb < 2 else "k"), (cb % 2) * N + c0
-            xc, xi = codes[xop, g]
+            xc, xi, x0 = codes[xop, g, tt // POS_TILES]
             xs, xsi = planes[xop, g]
-            wc, wi = codes[wop, g]
+            wc, wi, wc0 = codes[wop, g, cb % 2]
             ws, wsi = planes[wop, g]
             nc.tensor.matmul_mx(
                 out=acc[:, 0:width],
                 lhsT=xc[:, xi, 2 * P * col : 2 * P * (col + 1)].bitcast(FP4X4),
                 lhsT_scale=xs[:, xsi, P * col : P * (col + 1)],
-                rhs=wc[:, wi, 2 * n0 : 2 * (n0 + width)].bitcast(FP4X4),
+                rhs=wc[:, wi, 2 * (n0 - wc0) : 2 * (n0 - wc0 + width)].bitcast(FP4X4),
                 rhs_scale=ws[:, wsi, n0 : n0 + width],
                 start=(g == 0),
                 stop=(g == G - 1),
             )
 
-        pending = []
-
-        def finish(engine):
-            a, b, tt, cb, c0, width = pending.pop(0)
-            o = work.tile([P, N], F32, name="o")
-            engine.tensor_tensor(out=o[:, 0:width], in0=a[:, 0:width], in1=b[:, 0:width], op=ALU.add)
-            n0 = (cb % 2) * N + c0
-            nc.sync.dma_start(out=outs[cb // 2][P * tt : P * (tt + 1), n0 : n0 + width], in_=o[:, 0:width])
-
-        def rotate(acc, tt, cb, c0, width):
+        def tables(tt, width):
             heads = width // D
             m = tt % POS_TILES
             cosb = cos_t[:, m, :, :].rearrange("p j t -> p (j t)").unsqueeze(1).to_broadcast([P, heads, D])
             sinb = sin_t[:, m, :, :].unsqueeze(1).to_broadcast([P, heads, HALF, 2])
-            a = work.tile([P, N], F32, name="a")
-            b = work.tile([P, N], F32, name="b")
+            return cosb, sinb
+
+        pending = []
+
+        def products(src, tt, cb, c0, width):
+            cosb, sinb = tables(tt, width)
+            a = work.tile([P, C], F32, name="a")
+            b = work.tile([P, C], F32, name="b")
             nc.vector.tensor_tensor(
                 out=a[:, 0:width].rearrange("p (h d) -> p h d", d=D),
-                in0=acc[:, 0:width].rearrange("p (h d) -> p h d", d=D), in1=cosb, op=ALU.mult)
+                in0=src[:, 0:width].rearrange("p (h d) -> p h d", d=D), in1=cosb, op=ALU.mult)
             nc.vector.tensor_tensor(
                 out=b[:, 0:width].rearrange("p (h j t) -> p h j t", t=2, j=HALF),
-                in0=acc[:, 0:width].rearrange("p (h j t) -> p h j t", t=2, j=HALF)[:, :, :, ::-1], in1=sinb, op=ALU.mult)
+                in0=src[:, 0:width].rearrange("p (h j t) -> p h j t", t=2, j=HALF)[:, :, :, ::-1], in1=sinb, op=ALU.mult)
             pending.append((a, b, tt, cb, c0, width))
+
+        def finish(engine):
+            a, b, tt, cb, c0, width = pending.pop(0)
+            o = store.tile([P, C], F32, name="o")
+            engine.tensor_tensor(out=o[:, 0:width], in0=a[:, 0:width], in1=b[:, 0:width], op=ALU.add)
+            n0 = (cb % 2) * N + c0
+            nc.sync.dma_start(out=outs[cb // 2][P * tt : P * (tt + 1), n0 : n0 + width], in_=o[:, 0:width])
+
+        def rotate_pair(acc0, acc1, tt, cb):
+            s = stage.tile([P, C], F32, name="s")
+            nc.scalar.copy(out=s[:, 0:N], in_=acc0[:])
+            nc.scalar.copy(out=s[:, N:C], in_=acc1[:])
+            products(s, tt, cb, 0, C)
+            if len(pending) > 1:
+                finish(nc.vector)
 
         def new_acc():
             return psum.tile([P, N], F32, name="acc")
 
-        first = [(tt, cb) for tt in range(POS_TILES) for cb in range(2)]
+        warm = new_acc()
+        for i in range(10):
+            nc.tensor.matmul(warm[:], dummy[:, 0:P], dummy[:], start=True, stop=True)
+
+        first = [(tt, cb) for cb in range(2) for tt in range(POS_TILES)]
         accs = [new_acc() for pair in first]
         for g in range(G):
             for acc, (tt, cb) in zip(accs, first):
                 matmul(acc, tt, cb, 0, N, g)
-        for acc, (tt, cb) in zip(accs, first):
-            rotate(acc, tt, cb, 0, N)
-            if len(pending) > 1:
-                finish(nc.vector)
+        for tt in range(POS_TILES):
+            rotate_pair(accs[tt], accs[POS_TILES + tt], tt, 0)
 
-        rest = [(tt, cb) for tt in range(POS_TILES) for cb in range(2, 4)]
-        rest += [(tt, cb) for tt in range(POS_TILES, TOKENS // P) for cb in range(4)]
-        widths = {rest[-2]: [256, 256], rest[-1]: [256, 128, 128]}
-        for i, (tt, cb) in enumerate(rest):
-            c0 = 0
-            for width in widths.get((tt, cb), [N]):
-                acc = new_acc()
+        rest = [(tt, 2) for tt in range(POS_TILES)]
+        rest += [(tt, cb) for tt in range(POS_TILES, TOKENS // P) for cb in (0, 2)]
+        for tt, cb in rest[:-4]:
+            accs = [new_acc(), new_acc()]
+            for h in range(2):
                 for g in range(G):
-                    matmul(acc, tt, cb, c0, width, g)
-                rotate(acc, tt, cb, c0, width)
-                c0 += width
-                tail = i >= len(rest) - 3
-                if tail:
-                    while len(pending) > 1:
-                        finish(nc.vector)
-                    finish(nc.vector if (i == len(rest) - 1 and c0 == N) else nc.gpsimd)
-                elif len(pending) > 1:
-                    finish(nc.vector)
+                    matmul(accs[h], tt, cb + h, 0, N, g)
+            rotate_pair(accs[0], accs[1], tt, cb)
+        finish(nc.vector)
+        pieces = [(tt, cb + h, 0, N) for tt, cb in rest[-4:] for h in range(2)]
+        tt, cb = rest[-1]
+        pieces[-2:] = [(tt, cb, 0, 256), (tt, cb, 256, 256), (tt, cb + 1, 0, 256), (tt, cb + 1, 256, 128), (tt, cb + 1, 384, 128)]
+        for piece in pieces:
+            tt, cb, c0, width = piece
+            acc = new_acc()
+            for g in range(G):
+                matmul(acc, tt, cb, c0, width, g)
+            products(acc, tt, cb, c0, width)
+            finish(nc.vector if piece == pieces[-1] else nc.gpsimd)

import math
from contextlib import ExitStack

import concourse.mybir as mybir

F32 = mybir.dt.float32
I32 = mybir.dt.int32
U8 = mybir.dt.uint8
BF16 = mybir.dt.bfloat16
FP4X4 = mybir.dt.float4_e2m1fn_x4
ALU = mybir.AluOpType
SIN = mybir.ActivationFunctionType.Sin

B, S, E, NH, D = 4, 512, 4096, 16, 64
TOKENS = B * S
C = NH * D
BASE = 10000.0
FLOPS = 2 * TOKENS * E * 2 * C

P = 128
G = E // 512
N = 512
HALF = D // 2
POS_TILES = S // P


def load_codes(nc, dst, words, g0, g1, c0, c1):
    src = words[g0:g1, :, 2 * c0 : 2 * c1].rearrange("g p c -> p g c")
    nc.sync.dma_start(out=dst[:].bitcast(I32), in_=src.bitcast(I32))


def load_scales(nc, dst, scales, g0, g1, c0, c1):
    for q in range(4):
        src = scales[g0:g1, 4 * q : 4 * q + 4, c0:c1].rearrange("g r n -> r g n")
        nc.sync.dma_start(out=dst[32 * q : 32 * q + 4, :, :].bitcast(I32), in_=src.bitcast(I32))


def tile_multiheadflashdiff_pa_kernel(tc, x_words, x_scales, wq_words, wq_scales, wk_words, wk_scales, out_q, out_k):
    nc = tc.nc
    outs = [out_q.rearrange("b s h d -> (b s) (h d)"), out_k.rearrange("b s h d -> (b s) (h d)")]

    with ExitStack() as ctx:
        keep = ctx.enter_context(tc.tile_pool(name="keep", bufs=1))
        work = ctx.enter_context(tc.tile_pool(name="work", bufs=3))
        store = ctx.enter_context(tc.tile_pool(name="store", bufs=5))
        stage = ctx.enter_context(tc.tile_pool(name="stage", bufs=6))
        psum = ctx.enter_context(tc.psum_pool(name="psum", bufs=8))
        ctx.enter_context(tc.manual_schedule())

        def keep_tile(shape, dtype, name):
            return keep.tile(shape, dtype, name=name, align_bytes=256)

        codes = {}
        planes = {}

        def make_codes(op, words, g0, g1, c0, c1):
            t = keep_tile([P, g1 - g0, 2 * (c1 - c0)], U8, "codes_%s_%d_%d" % (op, g0, c0))
            load_codes(nc, t, words, g0, g1, c0, c1)
            for g in range(g0, g1):
                for c in range(c0, c1, N):
                    codes[op, g, c // N] = (t, g - g0, c0)

        def make_planes(op, g0, g1, c0, c1):
            t = keep_tile([P, g1 - g0, c1 - c0], U8, "planes_%s_%d_%d" % (op, g0, c0))
            nc.vector.memset(t[:].bitcast(I32), 0)
            for g in range(g0, g1):
                planes[op, g] = (t, g - g0)
            return t

        pos = keep_tile([P, POS_TILES, 1], F32, "pos")
        nc.gpsimd.iota(pos[:], [[P, POS_TILES], [1, 1]], base=0, channel_multiplier=1, allow_small_or_imprecise_dtypes=True)
        xp0 = make_planes("x0", 0, 4, 0, S)
        dummy = keep_tile([P, N], BF16, "dummy")
        nc.vector.memset(dummy[:].bitcast(I32), 0)
        qp0 = make_planes("q", 0, 2, 0, C)
        qp1 = make_planes("q", 2, 4, 0, C)
        xp1 = make_planes("x0", 4, G, 0, S)
        qp2 = make_planes("q", 4, G, 0, C)

        make_codes("x0", x_words, 0, 1, 0, S)
        make_codes("q", wq_words, 0, 1, 0, N)
        load_scales(nc, xp0, x_scales, 0, 4, 0, S)
        load_scales(nc, qp0, wq_scales, 0, 2, 0, C)
        make_codes("q", wq_words, 0, 1, N, C)
        make_codes("x0", x_words, 1, 2, 0, S)
        make_codes("q", wq_words, 1, 2, 0, C)
        make_codes("x0", x_words, 2, 4, 0, S)
        make_codes("q", wq_words, 2, 4, 0, C)
        load_scales(nc, qp1, wq_scales, 2, 4, 0, C)
        make_codes("x0", x_words, 4, G, 0, S)
        make_codes("q", wq_words, 4, 6, 0, C)
        load_scales(nc, xp1, x_scales, 4, G, 0, S)
        load_scales(nc, qp2, wq_scales, 4, G, 0, C)
        make_codes("q", wq_words, 6, G, 0, C)

        turns = keep_tile([P, 2, POS_TILES, HALF], F32, "turns")
        whole = keep_tile([P, 2, POS_TILES, HALF], I32, "whole")
        frac = keep_tile([P, 2, POS_TILES, HALF], F32, "frac")
        cos_t = keep_tile([P, POS_TILES, HALF, 2], F32, "cos_t")
        sin_t = keep_tile([P, POS_TILES, HALF, 2], F32, "sin_t")
        nc.vector.tensor_scalar(out=turns[:, 0, :, 0:1], in0=pos[:], scalar1=1.0 / (2.0 * math.pi), scalar2=None, op0=ALU.mult)
        w = 1
        while w < HALF:
            nc.vector.tensor_scalar(out=turns[:, 0, :, w : 2 * w], in0=turns[:, 0, :, 0:w], scalar1=BASE ** (-w / HALF), scalar2=None, op0=ALU.mult)
            w = 2 * w
        nc.vector.tensor_scalar(out=turns[:, 1, :, :], in0=turns[:, 0, :, :], scalar1=0.25, scalar2=None, op0=ALU.add)
        nc.vector.tensor_copy(out=whole[:], in_=turns[:])
        nc.vector.tensor_tensor(out=frac[:], in0=turns[:], in1=whole[:], op=ALU.subtract)
        two_pi = 2.0 * math.pi
        for t in range(2):
            nc.scalar.activation(out=cos_t[:, :, :, t], in_=frac[:, 1, :, :], func=SIN, scale=two_pi)
            nc.scalar.activation(out=sin_t[:, :, :, t], in_=frac[:, 0, :, :], func=SIN, scale=(two_pi if t == 1 else -two_pi))

        kp = make_planes("k", 0, G, 0, C)
        load_scales(nc, kp, wk_scales, 0, G, 0, C)
        for g in range(0, G, 2):
            make_codes("k", wk_words, g, g + 2, 0, C)
        rp = make_planes("x1", 0, G, S, TOKENS)
        load_scales(nc, rp, x_scales, 0, G, S, TOKENS)
        for g in range(0, G, 2):
            make_codes("x1", x_words, g, g + 2, S, TOKENS)

        def matmul(acc, tt, cb, c0, width, g):
            xop, col = ("x0", tt) if tt < POS_TILES else ("x1", tt - POS_TILES)
            wop, n0 = ("q" if cb < 2 else "k"), (cb % 2) * N + c0
            xc, xi, x0 = codes[xop, g, tt // POS_TILES]
            xs, xsi = planes[xop, g]
            wc, wi, wc0 = codes[wop, g, cb % 2]
            ws, wsi = planes[wop, g]
            nc.tensor.matmul_mx(
                out=acc[:, 0:width],
                lhsT=xc[:, xi, 2 * P * col : 2 * P * (col + 1)].bitcast(FP4X4),
                lhsT_scale=xs[:, xsi, P * col : P * (col + 1)],
                rhs=wc[:, wi, 2 * (n0 - wc0) : 2 * (n0 - wc0 + width)].bitcast(FP4X4),
                rhs_scale=ws[:, wsi, n0 : n0 + width],
                start=(g == 0),
                stop=(g == G - 1),
            )

        def tables(tt, width):
            heads = width // D
            m = tt % POS_TILES
            cosb = cos_t[:, m, :, :].rearrange("p j t -> p (j t)").unsqueeze(1).to_broadcast([P, heads, D])
            sinb = sin_t[:, m, :, :].unsqueeze(1).to_broadcast([P, heads, HALF, 2])
            return cosb, sinb

        pending = []

        def products(src, tt, cb, c0, width):
            cosb, sinb = tables(tt, width)
            a = work.tile([P, C], F32, name="a")
            b = work.tile([P, C], F32, name="b")
            nc.vector.tensor_tensor(
                out=a[:, 0:width].rearrange("p (h d) -> p h d", d=D),
                in0=src[:, 0:width].rearrange("p (h d) -> p h d", d=D), in1=cosb, op=ALU.mult)
            nc.vector.tensor_tensor(
                out=b[:, 0:width].rearrange("p (h j t) -> p h j t", t=2, j=HALF),
                in0=src[:, 0:width].rearrange("p (h j t) -> p h j t", t=2, j=HALF)[:, :, :, ::-1], in1=sinb, op=ALU.mult)
            pending.append((a, b, tt, cb, c0, width))

        def finish(engine):
            a, b, tt, cb, c0, width = pending.pop(0)
            o = store.tile([P, C], F32, name="o")
            engine.tensor_tensor(out=o[:, 0:width], in0=a[:, 0:width], in1=b[:, 0:width], op=ALU.add)
            n0 = (cb % 2) * N + c0
            nc.sync.dma_start(out=outs[cb // 2][P * tt : P * (tt + 1), n0 : n0 + width], in_=o[:, 0:width])

        def rotate_pair(acc0, acc1, tt, cb):
            s = stage.tile([P, C], F32, name="s")
            nc.scalar.copy(out=s[:, 0:N], in_=acc0[:])
            nc.scalar.copy(out=s[:, N:C], in_=acc1[:])
            products(s, tt, cb, 0, C)
            if len(pending) > 1:
                finish(nc.vector)

        def new_acc():
            return psum.tile([P, N], F32, name="acc")

        warm = new_acc()
        for i in range(10):
            nc.tensor.matmul(warm[:], dummy[:, 0:P], dummy[:], start=True, stop=True)

        first = [(tt, cb) for cb in range(2) for tt in range(POS_TILES)]
        accs = [new_acc() for pair in first]
        for g in range(G):
            for acc, (tt, cb) in zip(accs, first):
                matmul(acc, tt, cb, 0, N, g)
        for tt in range(POS_TILES):
            rotate_pair(accs[tt], accs[POS_TILES + tt], tt, 0)

        rest = [(tt, 2) for tt in range(POS_TILES)]
        rest += [(tt, cb) for tt in range(POS_TILES, TOKENS // P) for cb in (0, 2)]
        for tt, cb in rest[:-4]:
            accs = [new_acc(), new_acc()]
            for h in range(2):
                for g in range(G):
                    matmul(accs[h], tt, cb + h, 0, N, g)
            rotate_pair(accs[0], accs[1], tt, cb)
        finish(nc.vector)
        pieces = [(tt, cb + h, 0, N) for tt, cb in rest[-4:] for h in range(2)]
        tt, cb = rest[-1]
        pieces[-2:] = [(tt, cb, 0, 256), (tt, cb, 256, 256), (tt, cb + 1, 0, 256), (tt, cb + 1, 256, 128), (tt, cb + 1, 384, 128)]
        for piece in pieces:
            tt, cb, c0, width = piece
            acc = new_acc()
            for g in range(G):
                matmul(acc, tt, cb, c0, width, g)
            products(acc, tt, cb, c0, width)
            finish(nc.vector if piece == pieces[-1] else nc.gpsimd)
